import numpy as np
import ml_dtypes


def mxq(x, axis, fmt="e4m3"):
    dtype, down = {"e4m3": (ml_dtypes.float8_e4m3fn, 7), "e5m2": (ml_dtypes.float8_e5m2, 14)}[fmt]
    v = np.moveaxis(np.asarray(x, np.float32).astype(ml_dtypes.bfloat16).astype(np.float64), axis, -1)
    blocks = v.reshape(v.shape[:-1] + (-1, 32))
    amax = np.abs(blocks).max(-1, keepdims=True)
    byte = np.maximum(np.where(amax > 0, np.frexp(amax)[1] - 1 + 127, 0) - down, 1)
    scale = np.exp2(byte - 127.0)
    codes = (blocks / scale).astype(np.float32).astype(dtype).astype(np.float64)
    return np.moveaxis((codes * scale).reshape(v.shape), -1, axis)


WIDE = False


def mx_kscale(k):
    if not WIDE:
        return np.ones(k)
    levels = np.array([10, -10, 5, -5, 0])
    a = np.random.permutation(np.resize(levels, k // 512 * 4)).reshape(k // 512, 4)
    idx = np.arange(k)
    return np.exp2(a[idx // 512, idx % 128 // 32])


BF16 = ml_dtypes.bfloat16


def bf(x):
    return np.asarray(x, np.float32).astype(BF16)


def f64(x):
    return np.asarray(x).astype(np.float64)


B, D, E, H, W, SHIFT = 4, 1024, 1024, 16, 16, 5
EPS = 1e-5


def erf(v):
    a = np.clip(v, -6.0, 6.0)
    a2 = 2.0 * a * a
    term = a.copy()
    tot = a.copy()
    for n in range(120):
        term = term * a2 / (2 * n + 3)
        tot = tot + term
    return 2.0 / np.sqrt(np.pi) * np.exp(-a * a) * tot


def gelu(v):
    return 0.5 * v * (1.0 + erf(v / np.sqrt(2.0)))


def conv1x1(x, w, b):
    n, c, hh, ww = x.shape
    y = mxq(w, 1, "e4m3") @ mxq(x.reshape(n, c, hh * ww), 1, "e4m3")
    return y.reshape(n, -1, hh, ww) + b[None, :, None, None]


def group_norm1(x, gamma, beta):
    m = x.mean(axis=(1, 2, 3), keepdims=True)
    v = x.var(axis=(1, 2, 3), keepdims=True)
    xh = (x - m) / np.sqrt(v + EPS)
    return xh * gamma[None, :, None, None] + beta[None, :, None, None]


def setup_inputs():
    s = mx_kscale(D)
    return {"x": bf(np.random.standard_normal((B, D, H, W)) * s[None, :, None, None]),
            "w1": bf(np.random.standard_normal((E, D)) / np.sqrt(D) / s[None, :]),
            "b1": bf(np.random.standard_normal(E) * 0.3),
            "g1": bf(1.0 + 0.1 * np.random.standard_normal(E)),
            "be1": bf(0.2 * np.random.standard_normal(E))}


def reference(x, w1, b1, g1, be1):
    y = conv1x1(f64(x), f64(w1), f64(b1))
    return gelu(group_norm1(y, f64(g1), f64(be1)))

@@ -1,0 +1,343 @@
+from contextlib import ExitStack
+
+import concourse.mybir as mybir
+from concourse.masks import make_identity
+
+F32 = mybir.dt.float32
+BF16 = mybir.dt.bfloat16
+U32 = mybir.dt.uint32
+U8 = mybir.dt.uint8
+FP8X4 = mybir.dt.float8_e4m3fn_x4
+ALU = mybir.AluOpType
+ACT = mybir.ActivationFunctionType
+AX = mybir.AxisListType
+
+FLOPS = 2 * 1024 * 1024 * 1024
+
+P = 128
+NS = 4
+NT = 8
+NB = 4
+PIX = 256
+EPS = 1e-5
+
+
+def tile_axialshift_pa_kernel(tc, x, w1, b1, g1, be1, out):
+    nc = tc.nc
+    with ExitStack() as ctx:
+        keep = ctx.enter_context(tc.tile_pool(name="keep", bufs=1))
+        psum = ctx.enter_context(tc.psum_pool(name="psum", bufs=1))
+        ctx.enter_context(tc.manual_schedule())
+
+        w_sb = keep.tile([P, NT, 1024], BF16)
+        x_sb = keep.tile([P, NS, 2, 4, PIX], BF16)
+        wg = keep.tile([P, NT, 2, P, 4], BF16, align_bytes=64)
+        xg = keep.tile([P, NS, 2, PIX, 4], BF16, align_bytes=64)
+        wc = keep.tile([P, NT, 2 * P], U32, align_bytes=64)
+        ws = keep.tile([P, NT, 2 * P], U8, align_bytes=64)
+        xc = keep.tile([P, NS, 2 * PIX], U32, align_bytes=64)
+        xs = keep.tile([P, NS, 2 * PIX], U8, align_bytes=64)
+        o_sb = keep.tile([P, NS, NT, PIX], F32)
+        y_sb = keep.tile([P, NS, NB, 2, PIX], F32)
+
+        ident = keep.tile([P, P], F32)
+        cmat = keep.tile([P, P], F32)
+        epsrow = keep.tile([P, 4], F32)
+        brhs = keep.tile([P, 4], F32)
+        mhalf = keep.tile([P, 1], F32)
+        junk_in = keep.tile([P, 1], F32)
+        junk_out = keep.tile([P, 1], F32)
+        b_bf = keep.tile([P, NT], BF16)
+        g_bf = keep.tile([P, NT], BF16)
+        be_bf = keep.tile([P, NT], BF16)
+        b32 = keep.tile([P, NT], F32)
+        nmb = keep.tile([P, 1], F32)
+        bp_t = keep.tile([P, NT], F32)
+        stt = keep.tile([P, NS, NB, 6], F32)
+        rr = keep.tile([P, NS, 8], F32)
+        gu = keep.tile([P, NS, 2, NT], F32)
+        zb = keep.tile([P, 2, NT], F32)
+        sb = keep.tile([P, NS, 2, NT], F32)
+        ve = [keep.tile([P, 1], F32, name="ve%d" % n) for n in range(NS)]
+        rstd = [keep.tile([P, 1], F32, name="rstd%d" % n) for n in range(NS)]
+
+        w_view = w1.rearrange("(p t) k -> p t k", t=NT)
+        o_view = [out[n].rearrange("(p t) h w -> p t (h w)", t=NT) for n in range(NS)]
+        wt_tiles = {}
+        y_tiles = {}
+        ps_tiles = {}
+
+        def bank(k, shape, name):
+            return psum.tile(shape, F32, tag="bk%d" % k, name=name)
+
+        def params():
+            nc.scalar.dma_start(out=b_bf[:], in_=b1.rearrange("(p t) -> p t", t=NT))
+            nc.scalar.dma_start(out=g_bf[:], in_=g1.rearrange("(p t) -> p t", t=NT))
+            nc.scalar.dma_start(out=be_bf[:], in_=be1.rearrange("(p t) -> p t", t=NT))
+            nc.vector.memset(junk_in[:], 0.0)
+            nc.scalar.activation(out=junk_out[:], in_=junk_in[:], func=ACT.Gelu)
+            make_identity(nc, ident[:])
+            nc.vector.memset(cmat[:], 1.0 / P)
+            nc.vector.memset(epsrow[:], 0.0)
+            nc.vector.memset(epsrow[:, 3:4], EPS)
+            nc.vector.memset(brhs[:], 0.0)
+            nc.vector.memset(mhalf[:], -0.5)
+            nc.vector.memset(rr[:], 0.0)
+            nc.vector.memset(rr[:, :, 1:2], -1.0)
+            nc.vector.memset(zb[:], 0.0)
+
+        def lw(t):
+            nc.sync.dma_start(out=w_sb[:, t, :], in_=w_view[:, t, :])
+
+        def lx(n):
+            nc.sync.dma_start(
+                out=x_sb[:, n].rearrange("p g (u e) w -> p (g u) (e w)", e=2),
+                in_=x[n].rearrange("(a q e) h w -> q a (e h w)", a=4, q=P, e=2),
+            )
+
+        def cvt():
+            nc.vector.tensor_copy(out=b32[:], in_=b_bf[:])
+            nc.vector.tensor_copy(out=gu[:, :, 0, :],
+                                  in_=g_bf[:].unsqueeze(1).to_broadcast([P, NS, NT]))
+            nc.vector.tensor_copy(out=zb[:, 1, :], in_=be_bf[:])
+            nc.vector.tensor_reduce(out=brhs[:, 0:1], in_=b32[:], axis=AX.X, op=ALU.add)
+
+        def mmb(k):
+            psb = bank(k, [P, 4], "psb")
+            ps_tiles["b"] = psb
+            nc.tensor.matmul(psb[:], lhsT=cmat[:], rhs=brhs[:], start=True, stop=True)
+
+        def bp():
+            nc.vector.tensor_scalar(out=nmb[:], in0=ps_tiles["b"][:, 0:1], scalar1=-1.0 / NT,
+                                    scalar2=None, op0=ALU.mult)
+            nc.vector.tensor_scalar(out=bp_t[:], in0=b32[:], scalar1=nmb[:], scalar2=None,
+                                    op0=ALU.add)
+
+        def wT(t, k):
+            wt = bank(k, [P, 4, P], "wt%d" % t)
+            wt_tiles[t] = wt
+            words = w_sb[:, t, :].bitcast(F32)
+            for a in range(4):
+                nc.tensor.transpose(wt[:, a, :], words[:, a * P:(a + 1) * P], ident[:])
+
+        def wC(t, eng="S"):
+            dst = wg[:, t].rearrange("p g o s -> p (g o s)").bitcast(F32)
+            dst = dst.rearrange("p (g o u) -> p g o u", g=2, u=2)
+            src = wt_tiles[t][:].rearrange("p (g u) o -> p g o u", g=2)
+            if eng == "S":
+                nc.scalar.copy(out=dst, in_=src)
+            else:
+                nc.vector.tensor_copy(out=dst, in_=src)
+
+        def wQ(t):
+            nc.vector.quantize_mx(
+                out=wc[:, t, :].bitcast(FP8X4),
+                scales=ws[:, t, :],
+                in_=wg[:, t].rearrange("p g o s -> p (g o s)"),
+            )
+
+        def xR(n, g, eng):
+            dst = xg[:, n, g].rearrange("p (c i) s -> p c s i", i=4)
+            src = x_sb[:, n, g].rearrange("p s (c i) -> p c s i", i=4)
+            if eng == "V":
+                nc.vector.tensor_copy(out=dst, in_=src)
+            elif eng == "S":
+                nc.scalar.copy(out=dst, in_=src)
+            else:
+                nc.gpsimd.tensor_scalar(out=dst, in0=src, scalar1=1.0, scalar2=0.0,
+                                        op0=ALU.mult, op1=ALU.add)
+
+        def xQ(n):
+            nc.vector.quantize_mx(
+                out=xc[:, n, :].bitcast(FP8X4),
+                scales=xs[:, n, :],
+                in_=xg[:, n].rearrange("p g w s -> p (g w s)"),
+            )
+
+        def mx(n, b, k):
+            yb = bank(k, [P, 2, PIX], "y%d_%d" % (n, b))
+            y_tiles[(n, b)] = yb
+            for h in range(2):
+                t = 2 * b + h
+                for g in range(2):
+                    nc.tensor.matmul_mx(
+                        out=yb[:, h, :],
+                        lhsT=wc[:, t, g * P:(g + 1) * P].bitcast(FP8X4),
+                        lhsT_scale=ws[:, t, g * P:(g + 1) * P],
+                        rhs=xc[:, n, g * PIX:(g + 1) * PIX].bitcast(FP8X4),
+                        rhs_scale=xs[:, n, g * PIX:(g + 1) * PIX],
+                        start=(g == 0),
+                        stop=(g == 1),
+                    )
+
+        def st(n, b):
+            nc.vector.bn_stats(out=stt[:, n, b, :],
+                               in_=y_tiles[(n, b)][:].rearrange("p h w -> p w h"))
+
+        def ev(n, b, eng="V"):
+            if eng == "V":
+                nc.vector.tensor_copy(out=y_sb[:, n, b], in_=y_tiles[(n, b)][:])
+            else:
+                nc.scalar.copy(out=y_sb[:, n, b], in_=y_tiles[(n, b)][:])
+            y_tiles[(n, b)] = y_sb[:, n, b]
+
+        def V123(n):
+            means = stt[:, n].rearrange("p b (h s) -> p (b h) s", s=3)[:, :, 1]
+            nc.vector.tensor_tensor(out=means, in0=means, in1=bp_t[:], op=ALU.add)
+            nc.vector.bn_aggr(out=rr[:, n, 2:4], in_=stt[:, n].rearrange("p b s -> p (b s)"))
+            nc.vector.scalar_tensor_tensor(
+                out=rr[:, n, 4:6], in0=rr[:, n, 1:3], scalar=rr[:, n, 2:3],
+                in1=rr[:, n, 0:4:3], op0=ALU.mult, op1=ALU.add)
+
+        def mmE(n, k):
+            ps = bank(k, [P, 4], "ps%d" % n)
+            ps_tiles[n] = ps
+            nc.tensor.matmul(ps[:], lhsT=cmat[:], rhs=epsrow[:], start=True, stop=False)
+
+        def mmS(n):
+            nc.tensor.matmul(ps_tiles[n][:], lhsT=cmat[:], rhs=rr[:, n, 2:6], start=False, stop=True)
+
+        def Vau(n):
+            ps = ps_tiles[n]
+            nc.vector.tensor_scalar(out=ve[n][:], in0=ps[:, 0:1], scalar1=ps[:, 2:3],
+                                    scalar2=ps[:, 3:4], op0=ALU.mult, op1=ALU.add)
+            nc.gpsimd.tensor_tensor(out=rstd[n][:], in0=ve[n][:], in1=mhalf[:], op=ALU.pow)
+            nc.vector.scalar_tensor_tensor(
+                out=gu[:, n, 1, :], in0=bp_t[:], scalar=ps[:, 2:3], in1=gu[:, n, 0, :],
+                op0=ALU.add, op1=ALU.mult)
+
+        def Vs(n):
+            nc.vector.scalar_tensor_tensor(
+                out=sb[:, n].rearrange("p a t -> p (a t)"),
+                in0=gu[:, n].rearrange("p a t -> p (a t)"), scalar=rstd[n][:],
+                in1=zb[:].rearrange("p a t -> p (a t)"), op0=ALU.mult, op1=ALU.add)
+
+        def ge(n, b):
+            yb = y_tiles[(n, b)]
+            for h in range(2):
+                t = 2 * b + h
+                nc.scalar.activation(out=o_sb[:, n, t, :], in_=yb[:, h, :], func=ACT.Gelu,
+                                     scale=sb[:, n, 0, t:t + 1], bias=sb[:, n, 1, t:t + 1])
+            nc.sync.dma_start(out=o_view[n][:, 2 * b:2 * b + 2, :],
+                              in_=o_sb[:, n, 2 * b:2 * b + 2, :])
+
+        params()
+        lx(0)
+        lx(1)
+        lw(0)
+        lw(1)
+        lw(2)
+        lw(3)
+        lw(4)
+        lw(5)
+        lw(6)
+        lw(7)
+        lx(2)
+        lx(3)
+        xR(0, 0, "V")
+        xR(0, 1, "V")
+        xQ(0)
+        xR(1, 0, "V")
+        xR(1, 1, "V")
+        xQ(1)
+        cvt()
+        wT(0, 4)
+        wC(0)
+        wT(1, 5)
+        wC(1)
+        wT(2, 6)
+        wC(2)
+        wT(3, 7)
+        wC(3)
+        mmb(3)
+        wQ(0)
+        wQ(1)
+        bp()
+        wT(4, 4)
+        wC(4)
+        wT(5, 5)
+        wC(5)
+        wQ(2)
+        wQ(3)
+        mx(0, 0, 0)
+        wT(6, 6)
+        wC(6)
+        wT(7, 7)
+        wC(7)
+        st(0, 0)
+        wQ(4)
+        wQ(5)
+        wQ(6)
+        wQ(7)
+        mx(0, 1, 1)
+        mx(0, 2, 2)
+        mx(0, 3, 3)
+        st(0, 1)
+        st(0, 2)
+        st(0, 3)
+        xR(2, 0, "S")
+        xR(2, 1, "S")
+        xR(3, 0, "S")
+        xR(3, 1, "S")
+        mx(1, 0, 4)
+        mx(1, 1, 5)
+        mx(1, 2, 6)
+        mmE(0, 7)
+        V123(0)
+        mmS(0)
+        st(1, 0)
+        Vau(0)
+        mx(1, 3, 7)
+        xQ(2)
+        Vs(0)
+        st(1, 1)
+        st(1, 2)
+        st(1, 3)
+        ge(0, 0)
+        mx(2, 0, 0)
+        ge(0, 1)
+        mmE(1, 1)
+        V123(1)
+        mmS(1)
+        xQ(3)
+        Vau(1)
+        mx(2, 1, 1)
+        st(2, 0)
+        Vs(1)
+        ge(0, 2)
+        mx(2, 2, 2)
+        ge(0, 3)
+        mx(2, 3, 3)
+        st(2, 1)
+        st(2, 2)
+        st(2, 3)
+        ge(1, 0)
+        mx(3, 0, 4)
+        ge(1, 1)
+        mmE(2, 5)
+        V123(2)
+        mmS(2)
+        st(3, 0)
+        Vau(2)
+        mx(3, 1, 5)
+        Vs(2)
+        ge(1, 2)
+        mx(3, 2, 6)
+        ge(1, 3)
+        mx(3, 3, 7)
+        st(3, 1)
+        st(3, 2)
+        st(3, 3)
+        ge(2, 0)
+        mmE(3, 0)
+        V123(3)
+        mmS(3)
+        Vau(3)
+        Vs(3)
+        ge(2, 1)
+        ge(2, 2)
+        ge(2, 3)
+        ge(3, 0)
+        ge(3, 1)
+        ge(3, 2)
+        ge(3, 3)

@@ -38,11 +38,9 @@ def tile_axialshift_pa_kernel(tc, x, w1, b1, g1, be1, out):
         xc = keep.tile([P, NS, 2 * PIX], U32, align_bytes=64)
         xs = keep.tile([P, NS, 2 * PIX], U8, align_bytes=64)
         o_sb = keep.tile([P, NS, NT, PIX], F32)
-        y_sb = keep.tile([P, NS, NB, 2, PIX], F32)
 
         ident = keep.tile([P, P], F32)
         cmat = keep.tile([P, P], F32)
-        epsrow = keep.tile([P, 4], F32)
         brhs = keep.tile([P, 4], F32)
         mhalf = keep.tile([P, 1], F32)
         junk_in = keep.tile([P, 1], F32)
@@ -52,7 +50,7 @@ def tile_axialshift_pa_kernel(tc, x, w1, b1, g1, be1, out):
         be_bf = keep.tile([P, NT], BF16)
         b32 = keep.tile([P, NT], F32)
         nmb = keep.tile([P, 1], F32)
-        bp_t = keep.tile([P, NT], F32)
+        addc = keep.tile([P, NT, 2], F32)
         stt = keep.tile([P, NS, NB, 6], F32)
         rr = keep.tile([P, NS, 8], F32)
         gu = keep.tile([P, NS, 2, NT], F32)
@@ -78,8 +76,7 @@ def tile_axialshift_pa_kernel(tc, x, w1, b1, g1, be1, out):
             nc.scalar.activation(out=junk_out[:], in_=junk_in[:], func=ACT.Gelu)
             make_identity(nc, ident[:])
             nc.vector.memset(cmat[:], 1.0 / P)
-            nc.vector.memset(epsrow[:], 0.0)
-            nc.vector.memset(epsrow[:, 3:4], EPS)
+            nc.vector.memset(addc[:], PIX * EPS)
             nc.vector.memset(brhs[:], 0.0)
             nc.vector.memset(mhalf[:], -0.5)
             nc.vector.memset(rr[:], 0.0)
@@ -110,7 +107,7 @@ def tile_axialshift_pa_kernel(tc, x, w1, b1, g1, be1, out):
         def bp():
             nc.vector.tensor_scalar(out=nmb[:], in0=ps_tiles["b"][:, 0:1], scalar1=-1.0 / NT,
                                     scalar2=None, op0=ALU.mult)
-            nc.vector.tensor_scalar(out=bp_t[:], in0=b32[:], scalar1=nmb[:], scalar2=None,
+            nc.vector.tensor_scalar(out=addc[:, :, 0], in0=b32[:], scalar1=nmb[:], scalar2=None,
                                     op0=ALU.add)
 
         def wT(t, k):
@@ -174,28 +171,18 @@ def tile_axialshift_pa_kernel(tc, x, w1, b1, g1, be1, out):
             nc.vector.bn_stats(out=stt[:, n, b, :],
                                in_=y_tiles[(n, b)][:].rearrange("p h w -> p w h"))
 
-        def ev(n, b, eng="V"):
-            if eng == "V":
-                nc.vector.tensor_copy(out=y_sb[:, n, b], in_=y_tiles[(n, b)][:])
-            else:
-                nc.scalar.copy(out=y_sb[:, n, b], in_=y_tiles[(n, b)][:])
-            y_tiles[(n, b)] = y_sb[:, n, b]
-
         def V123(n):
-            means = stt[:, n].rearrange("p b (h s) -> p (b h) s", s=3)[:, :, 1]
-            nc.vector.tensor_tensor(out=means, in0=means, in1=bp_t[:], op=ALU.add)
+            pairs = stt[:, n].rearrange("p b (h s) -> p (b h) s", s=3)[:, :, 1:3]
+            nc.vector.tensor_tensor(out=pairs, in0=pairs, in1=addc[:], op=ALU.add)
             nc.vector.bn_aggr(out=rr[:, n, 2:4], in_=stt[:, n].rearrange("p b s -> p (b s)"))
             nc.vector.scalar_tensor_tensor(
                 out=rr[:, n, 4:6], in0=rr[:, n, 1:3], scalar=rr[:, n, 2:3],
                 in1=rr[:, n, 0:4:3], op0=ALU.mult, op1=ALU.add)
 
-        def mmE(n, k):
+        def mmS(n, k):
             ps = bank(k, [P, 4], "ps%d" % n)
             ps_tiles[n] = ps
-            nc.tensor.matmul(ps[:], lhsT=cmat[:], rhs=epsrow[:], start=True, stop=False)
-
-        def mmS(n):
-            nc.tensor.matmul(ps_tiles[n][:], lhsT=cmat[:], rhs=rr[:, n, 2:6], start=False, stop=True)
+            nc.tensor.matmul(ps[:], lhsT=cmat[:], rhs=rr[:, n, 2:6], start=True, stop=True)
 
         def Vau(n):
             ps = ps_tiles[n]
@@ -203,7 +190,7 @@ def tile_axialshift_pa_kernel(tc, x, w1, b1, g1, be1, out):
                                     scalar2=ps[:, 3:4], op0=ALU.mult, op1=ALU.add)
             nc.gpsimd.tensor_tensor(out=rstd[n][:], in0=ve[n][:], in1=mhalf[:], op=ALU.pow)
             nc.vector.scalar_tensor_tensor(
-                out=gu[:, n, 1, :], in0=bp_t[:], scalar=ps[:, 2:3], in1=gu[:, n, 0, :],
+                out=gu[:, n, 1, :], in0=addc[:, :, 0], scalar=ps[:, 2:3], in1=gu[:, n, 0, :],
                 op0=ALU.add, op1=ALU.mult)
 
         def Vs(n):
@@ -252,86 +239,82 @@ def tile_axialshift_pa_kernel(tc, x, w1, b1, g1, be1, out):
         mmb(3)
         wQ(0)
         wQ(1)
+        wQ(2)
+        wQ(3)
         bp()
         wT(4, 4)
         wC(4)
         wT(5, 5)
         wC(5)
-        wQ(2)
-        wQ(3)
-        mx(0, 0, 0)
         wT(6, 6)
         wC(6)
         wT(7, 7)
         wC(7)
-        st(0, 0)
         wQ(4)
         wQ(5)
         wQ(6)
         wQ(7)
-        mx(0, 1, 1)
-        mx(0, 2, 2)
-        mx(0, 3, 3)
-        st(0, 1)
-        st(0, 2)
-        st(0, 3)
         xR(2, 0, "S")
         xR(2, 1, "S")
         xR(3, 0, "S")
         xR(3, 1, "S")
+        mx(0, 0, 0)
+        mx(0, 1, 1)
+        mx(0, 2, 2)
+        mx(0, 3, 3)
+        st(0, 0)
+        st(0, 1)
+        st(0, 2)
+        st(0, 3)
         mx(1, 0, 4)
-        mx(1, 1, 5)
-        mx(1, 2, 6)
-        mmE(0, 7)
         V123(0)
-        mmS(0)
-        st(1, 0)
-        Vau(0)
-        mx(1, 3, 7)
+        mmS(0, 5)
         xQ(2)
-        Vs(0)
-        st(1, 1)
+        Vau(0)
+        mx(1, 2, 6)
+        mx(1, 3, 7)
+        mx(1, 1, 5)
+        st(1, 0)
         st(1, 2)
+        Vs(0)
         st(1, 3)
+        st(1, 1)
         ge(0, 0)
         mx(2, 0, 0)
         ge(0, 1)
-        mmE(1, 1)
         V123(1)
-        mmS(1)
+        mmS(1, 1)
         xQ(3)
         Vau(1)
-        mx(2, 1, 1)
-        st(2, 0)
-        Vs(1)
         ge(0, 2)
         mx(2, 2, 2)
         ge(0, 3)
         mx(2, 3, 3)
-        st(2, 1)
+        mx(2, 1, 1)
+        st(2, 0)
         st(2, 2)
+        Vs(1)
         st(2, 3)
+        st(2, 1)
         ge(1, 0)
         mx(3, 0, 4)
         ge(1, 1)
-        mmE(2, 5)
         V123(2)
-        mmS(2)
+        mmS(2, 5)
         st(3, 0)
         Vau(2)
-        mx(3, 1, 5)
-        Vs(2)
         ge(1, 2)
         mx(3, 2, 6)
         ge(1, 3)
         mx(3, 3, 7)
-        st(3, 1)
+        mx(3, 1, 5)
         st(3, 2)
         st(3, 3)
+        Vs(2)
+        st(3, 1)
         ge(2, 0)
-        mmE(3, 0)
         V123(3)
-        mmS(3)
+        mmS(3, 0)
         Vau(3)
         Vs(3)
         ge(2, 1)

@@ -43,6 +43,7 @@ def tile_axialshift_pa_kernel(tc, x, w1, b1, g1, be1, out):
         cmat = keep.tile([P, P], F32)
         brhs = keep.tile([P, 4], F32)
         mhalf = keep.tile([P, 1], F32)
+        warm = keep.tile([P, 2 * P], F32)
         junk_in = keep.tile([P, 1], F32)
         junk_out = keep.tile([P, 1], F32)
         b_bf = keep.tile([P, NT], BF16)
@@ -72,16 +73,21 @@ def tile_axialshift_pa_kernel(tc, x, w1, b1, g1, be1, out):
             nc.scalar.dma_start(out=b_bf[:], in_=b1.rearrange("(p t) -> p t", t=NT))
             nc.scalar.dma_start(out=g_bf[:], in_=g1.rearrange("(p t) -> p t", t=NT))
             nc.scalar.dma_start(out=be_bf[:], in_=be1.rearrange("(p t) -> p t", t=NT))
+            nc.vector.memset(cmat[:], 1.0 / P)
+            nc.vector.memset(warm[:], 0.0)
             nc.vector.memset(junk_in[:], 0.0)
             nc.scalar.activation(out=junk_out[:], in_=junk_in[:], func=ACT.Gelu)
             make_identity(nc, ident[:])
-            nc.vector.memset(cmat[:], 1.0 / P)
             nc.vector.memset(addc[:], PIX * EPS)
             nc.vector.memset(brhs[:], 0.0)
             nc.vector.memset(mhalf[:], -0.5)
             nc.vector.memset(rr[:], 0.0)
             nc.vector.memset(rr[:, :, 1:2], -1.0)
             nc.vector.memset(zb[:], 0.0)
+
+        def heat(k, cols):
+            ht = bank(k, [P, cols], "heat")
+            nc.tensor.matmul(ht[:], lhsT=cmat[:], rhs=warm[:, 0:cols], start=True, stop=True)
 
         def lw(t):
             nc.sync.dma_start(out=w_sb[:, t, :], in_=w_view[:, t, :])
@@ -221,6 +227,13 @@ def tile_axialshift_pa_kernel(tc, x, w1, b1, g1, be1, out):
         lw(7)
         lx(2)
         lx(3)
+        heat(0, 256)
+        heat(0, 256)
+        heat(0, 256)
+        heat(0, 256)
+        heat(0, 256)
+        heat(0, 256)
+        heat(0, 256)
         xR(0, 0, "V")
         xR(0, 1, "V")
         xQ(0)
@@ -232,11 +245,13 @@ def tile_axialshift_pa_kernel(tc, x, w1, b1, g1, be1, out):
         wC(0)
         wT(1, 5)
         wC(1)
+        heat(0, 128)
         wT(2, 6)
         wC(2)
         wT(3, 7)
         wC(3)
         mmb(3)
+        heat(0, 128)
         wQ(0)
         wQ(1)
         wQ(2)
@@ -246,10 +261,12 @@ def tile_axialshift_pa_kernel(tc, x, w1, b1, g1, be1, out):
         wC(4)
         wT(5, 5)
         wC(5)
+        heat(0, 128)
         wT(6, 6)
         wC(6)
         wT(7, 7)
         wC(7)
+        heat(0, 128)
         wQ(4)
         wQ(5)
         wQ(6)

from contextlib import ExitStack

import concourse.mybir as mybir
from concourse.masks import make_identity

F32 = mybir.dt.float32
BF16 = mybir.dt.bfloat16
U32 = mybir.dt.uint32
U8 = mybir.dt.uint8
FP8X4 = mybir.dt.float8_e4m3fn_x4
ALU = mybir.AluOpType
ACT = mybir.ActivationFunctionType
AX = mybir.AxisListType

FLOPS = 2 * 1024 * 1024 * 1024

P = 128
NS = 4
NT = 8
NB = 4
PIX = 256
EPS = 1e-5


def tile_axialshift_pa_kernel(tc, x, w1, b1, g1, be1, out):
    nc = tc.nc
    with ExitStack() as ctx:
        keep = ctx.enter_context(tc.tile_pool(name="keep", bufs=1))
        psum = ctx.enter_context(tc.psum_pool(name="psum", bufs=1))
        ctx.enter_context(tc.manual_schedule())

        w_sb = keep.tile([P, NT, 1024], BF16)
        x_sb = keep.tile([P, NS, 2, 4, PIX], BF16)
        wg = keep.tile([P, NT, 2, P, 4], BF16, align_bytes=64)
        xg = keep.tile([P, NS, 2, PIX, 4], BF16, align_bytes=64)
        wc = keep.tile([P, NT, 2 * P], U32, align_bytes=64)
        ws = keep.tile([P, NT, 2 * P], U8, align_bytes=64)
        xc = keep.tile([P, NS, 2 * PIX], U32, align_bytes=64)
        xs = keep.tile([P, NS, 2 * PIX], U8, align_bytes=64)
        o_sb = keep.tile([P, NS, NT, PIX], F32)

        ident = keep.tile([P, P], F32)
        cmat = keep.tile([P, P], F32)
        brhs = keep.tile([P, 4], F32)
        mhalf = keep.tile([P, 1], F32)
        warm = keep.tile([P, 2 * P], F32)
        junk_in = keep.tile([P, 1], F32)
        junk_out = keep.tile([P, 1], F32)
        b_bf = keep.tile([P, NT], BF16)
        g_bf = keep.tile([P, NT], BF16)
        be_bf = keep.tile([P, NT], BF16)
        b32 = keep.tile([P, NT], F32)
        nmb = keep.tile([P, 1], F32)
        addc = keep.tile([P, NT, 2], F32)
        stt = keep.tile([P, NS, NB, 6], F32)
        rr = keep.tile([P, NS, 8], F32)
        gu = keep.tile([P, NS, 2, NT], F32)
        zb = keep.tile([P, 2, NT], F32)
        sb = keep.tile([P, NS, 2, NT], F32)
        ve = [keep.tile([P, 1], F32, name="ve%d" % n) for n in range(NS)]
        rstd = [keep.tile([P, 1], F32, name="rstd%d" % n) for n in range(NS)]

        w_view = w1.rearrange("(p t) k -> p t k", t=NT)
        o_view = [out[n].rearrange("(p t) h w -> p t (h w)", t=NT) for n in range(NS)]
        wt_tiles = {}
        y_tiles = {}
        ps_tiles = {}

        def bank(k, shape, name):
            return psum.tile(shape, F32, tag="bk%d" % k, name=name)

        def params():
            nc.scalar.dma_start(out=b_bf[:], in_=b1.rearrange("(p t) -> p t", t=NT))
            nc.scalar.dma_start(out=g_bf[:], in_=g1.rearrange("(p t) -> p t", t=NT))
            nc.scalar.dma_start(out=be_bf[:], in_=be1.rearrange("(p t) -> p t", t=NT))
            nc.vector.memset(cmat[:], 1.0 / P)
            nc.vector.memset(warm[:], 0.0)
            nc.vector.memset(junk_in[:], 0.0)
            nc.scalar.activation(out=junk_out[:], in_=junk_in[:], func=ACT.Gelu)
            make_identity(nc, ident[:])
            nc.vector.memset(addc[:], PIX * EPS)
            nc.vector.memset(brhs[:], 0.0)
            nc.vector.memset(mhalf[:], -0.5)
            nc.vector.memset(rr[:], 0.0)
            nc.vector.memset(rr[:, :, 1:2], -1.0)
            nc.vector.memset(zb[:], 0.0)

        def heat(k, cols):
            ht = bank(k, [P, cols], "heat")
            nc.tensor.matmul(ht[:], lhsT=cmat[:], rhs=warm[:, 0:cols], start=True, stop=True)

        def lw(t):
            nc.sync.dma_start(out=w_sb[:, t, :], in_=w_view[:, t, :])

        def lx(n):
            nc.sync.dma_start(
                out=x_sb[:, n].rearrange("p g (u e) w -> p (g u) (e w)", e=2),
                in_=x[n].rearrange("(a q e) h w -> q a (e h w)", a=4, q=P, e=2),
            )

        def cvt():
            nc.vector.tensor_copy(out=b32[:], in_=b_bf[:])
            nc.vector.tensor_copy(out=gu[:, :, 0, :],
                                  in_=g_bf[:].unsqueeze(1).to_broadcast([P, NS, NT]))
            nc.vector.tensor_copy(out=zb[:, 1, :], in_=be_bf[:])
            nc.vector.tensor_reduce(out=brhs[:, 0:1], in_=b32[:], axis=AX.X, op=ALU.add)

        def mmb(k):
            psb = bank(k, [P, 4], "psb")
            ps_tiles["b"] = psb
            nc.tensor.matmul(psb[:], lhsT=cmat[:], rhs=brhs[:], start=True, stop=True)

        def bp():
            nc.vector.tensor_scalar(out=nmb[:], in0=ps_tiles["b"][:, 0:1], scalar1=-1.0 / NT,
                                    scalar2=None, op0=ALU.mult)
            nc.vector.tensor_scalar(out=addc[:, :, 0], in0=b32[:], scalar1=nmb[:], scalar2=None,
                                    op0=ALU.add)

        def wT(t, k):
            wt = bank(k, [P, 4, P], "wt%d" % t)
            wt_tiles[t] = wt
            words = w_sb[:, t, :].bitcast(F32)
            for a in range(4):
                nc.tensor.transpose(wt[:, a, :], words[:, a * P:(a + 1) * P], ident[:])

        def wC(t, eng="S"):
            dst = wg[:, t].rearrange("p g o s -> p (g o s)").bitcast(F32)
            dst = dst.rearrange("p (g o u) -> p g o u", g=2, u=2)
            src = wt_tiles[t][:].rearrange("p (g u) o -> p g o u", g=2)
            if eng == "S":
                nc.scalar.copy(out=dst, in_=src)
            else:
                nc.vector.tensor_copy(out=dst, in_=src)

        def wQ(t):
            nc.vector.quantize_mx(
                out=wc[:, t, :].bitcast(FP8X4),
                scales=ws[:, t, :],
                in_=wg[:, t].rearrange("p g o s -> p (g o s)"),
            )

        def xR(n, g, eng):
            dst = xg[:, n, g].rearrange("p (c i) s -> p c s i", i=4)
            src = x_sb[:, n, g].rearrange("p s (c i) -> p c s i", i=4)
            if eng == "V":
                nc.vector.tensor_copy(out=dst, in_=src)
            elif eng == "S":
                nc.scalar.copy(out=dst, in_=src)
            else:
                nc.gpsimd.tensor_scalar(out=dst, in0=src, scalar1=1.0, scalar2=0.0,
                                        op0=ALU.mult, op1=ALU.add)

        def xQ(n):
            nc.vector.quantize_mx(
                out=xc[:, n, :].bitcast(FP8X4),
                scales=xs[:, n, :],
                in_=xg[:, n].rearrange("p g w s -> p (g w s)"),
            )

        def mx(n, b, k):
            yb = bank(k, [P, 2, PIX], "y%d_%d" % (n, b))
            y_tiles[(n, b)] = yb
            for h in range(2):
                t = 2 * b + h
                for g in range(2):
                    nc.tensor.matmul_mx(
                        out=yb[:, h, :],
                        lhsT=wc[:, t, g * P:(g + 1) * P].bitcast(FP8X4),
                        lhsT_scale=ws[:, t, g * P:(g + 1) * P],
                        rhs=xc[:, n, g * PIX:(g + 1) * PIX].bitcast(FP8X4),
                        rhs_scale=xs[:, n, g * PIX:(g + 1) * PIX],
                        start=(g == 0),
                        stop=(g == 1),
                    )

        def st(n, b):
            nc.vector.bn_stats(out=stt[:, n, b, :],
                               in_=y_tiles[(n, b)][:].rearrange("p h w -> p w h"))

        def V123(n):
            pairs = stt[:, n].rearrange("p b (h s) -> p (b h) s", s=3)[:, :, 1:3]
            nc.vector.tensor_tensor(out=pairs, in0=pairs, in1=addc[:], op=ALU.add)
            nc.vector.bn_aggr(out=rr[:, n, 2:4], in_=stt[:, n].rearrange("p b s -> p (b s)"))
            nc.vector.scalar_tensor_tensor(
                out=rr[:, n, 4:6], in0=rr[:, n, 1:3], scalar=rr[:, n, 2:3],
                in1=rr[:, n, 0:4:3], op0=ALU.mult, op1=ALU.add)

        def mmS(n, k):
            ps = bank(k, [P, 4], "ps%d" % n)
            ps_tiles[n] = ps
            nc.tensor.matmul(ps[:], lhsT=cmat[:], rhs=rr[:, n, 2:6], start=True, stop=True)

        def Vau(n):
            ps = ps_tiles[n]
            nc.vector.tensor_scalar(out=ve[n][:], in0=ps[:, 0:1], scalar1=ps[:, 2:3],
                                    scalar2=ps[:, 3:4], op0=ALU.mult, op1=ALU.add)
            nc.gpsimd.tensor_tensor(out=rstd[n][:], in0=ve[n][:], in1=mhalf[:], op=ALU.pow)
            nc.vector.scalar_tensor_tensor(
                out=gu[:, n, 1, :], in0=addc[:, :, 0], scalar=ps[:, 2:3], in1=gu[:, n, 0, :],
                op0=ALU.add, op1=ALU.mult)

        def Vs(n):
            nc.vector.scalar_tensor_tensor(
                out=sb[:, n].rearrange("p a t -> p (a t)"),
                in0=gu[:, n].rearrange("p a t -> p (a t)"), scalar=rstd[n][:],
                in1=zb[:].rearrange("p a t -> p (a t)"), op0=ALU.mult, op1=ALU.add)

        def ge(n, b):
            yb = y_tiles[(n, b)]
            for h in range(2):
                t = 2 * b + h
                nc.scalar.activation(out=o_sb[:, n, t, :], in_=yb[:, h, :], func=ACT.Gelu,
                                     scale=sb[:, n, 0, t:t + 1], bias=sb[:, n, 1, t:t + 1])
            nc.sync.dma_start(out=o_view[n][:, 2 * b:2 * b + 2, :],
                              in_=o_sb[:, n, 2 * b:2 * b + 2, :])

        params()
        lx(0)
        lx(1)
        lw(0)
        lw(1)
        lw(2)
        lw(3)
        lw(4)
        lw(5)
        lw(6)
        lw(7)
        lx(2)
        lx(3)
        heat(0, 256)
        heat(0, 256)
        heat(0, 256)
        heat(0, 256)
        heat(0, 256)
        heat(0, 256)
        heat(0, 256)
        xR(0, 0, "V")
        xR(0, 1, "V")
        xQ(0)
        xR(1, 0, "V")
        xR(1, 1, "V")
        xQ(1)
        cvt()
        wT(0, 4)
        wC(0)
        wT(1, 5)
        wC(1)
        heat(0, 128)
        wT(2, 6)
        wC(2)
        wT(3, 7)
        wC(3)
        mmb(3)
        heat(0, 128)
        wQ(0)
        wQ(1)
        wQ(2)
        wQ(3)
        bp()
        wT(4, 4)
        wC(4)
        wT(5, 5)
        wC(5)
        heat(0, 128)
        wT(6, 6)
        wC(6)
        wT(7, 7)
        wC(7)
        heat(0, 128)
        wQ(4)
        wQ(5)
        wQ(6)
        wQ(7)
        xR(2, 0, "S")
        xR(2, 1, "S")
        xR(3, 0, "S")
        xR(3, 1, "S")
        mx(0, 0, 0)
        mx(0, 1, 1)
        mx(0, 2, 2)
        mx(0, 3, 3)
        st(0, 0)
        st(0, 1)
        st(0, 2)
        st(0, 3)
        mx(1, 0, 4)
        V123(0)
        mmS(0, 5)
        xQ(2)
        Vau(0)
        mx(1, 2, 6)
        mx(1, 3, 7)
        mx(1, 1, 5)
        st(1, 0)
        st(1, 2)
        Vs(0)
        st(1, 3)
        st(1, 1)
        ge(0, 0)
        mx(2, 0, 0)
        ge(0, 1)
        V123(1)
        mmS(1, 1)
        xQ(3)
        Vau(1)
        ge(0, 2)
        mx(2, 2, 2)
        ge(0, 3)
        mx(2, 3, 3)
        mx(2, 1, 1)
        st(2, 0)
        st(2, 2)
        Vs(1)
        st(2, 3)
        st(2, 1)
        ge(1, 0)
        mx(3, 0, 4)
        ge(1, 1)
        V123(2)
        mmS(2, 5)
        st(3, 0)
        Vau(2)
        ge(1, 2)
        mx(3, 2, 6)
        ge(1, 3)
        mx(3, 3, 7)
        mx(3, 1, 5)
        st(3, 2)
        st(3, 3)
        Vs(2)
        st(3, 1)
        ge(2, 0)
        V123(3)
        mmS(3, 0)
        Vau(3)
        Vs(3)
        ge(2, 1)
        ge(2, 2)
        ge(2, 3)
        ge(3, 0)
        ge(3, 1)
        ge(3, 2)
        ge(3, 3)
